import numpy as np
import ml_dtypes


def mxq(x, axis, fmt="e4m3"):
    dtype, down = {"e4m3": (ml_dtypes.float8_e4m3fn, 7), "e5m2": (ml_dtypes.float8_e5m2, 14)}[fmt]
    v = np.moveaxis(np.asarray(x, np.float32).astype(ml_dtypes.bfloat16).astype(np.float64), axis, -1)
    blocks = v.reshape(v.shape[:-1] + (-1, 32))
    amax = np.abs(blocks).max(-1, keepdims=True)
    byte = np.maximum(np.where(amax > 0, np.frexp(amax)[1] - 1 + 127, 0) - down, 1)
    scale = np.exp2(byte - 127.0)
    codes = (blocks / scale).astype(np.float32).astype(dtype).astype(np.float64)
    return np.moveaxis((codes * scale).reshape(v.shape), -1, axis)


WIDE = False


def mx_kscale(k):
    if not WIDE:
        return np.ones(k)
    levels = np.array([18, -18])
    if k % 512:
        return np.exp2(np.random.permutation(np.resize(levels, k // 32))).repeat(32)
    a = np.empty((k // 512, 16))
    for p in range(k // 512):
        a[p, :8] = np.random.permutation(np.resize(levels, 8))
        for g in range(8):
            far = levels[np.abs(levels - a[p, g]) >= 10]
            a[p, g + 8] = far[np.random.randint(len(far))]
    return np.exp2(a.ravel()).repeat(32)


BF16 = ml_dtypes.bfloat16


def bf(x):
    return np.asarray(x, np.float32).astype(BF16)


def f64(x):
    return np.asarray(x).astype(np.float64)


B, S, D, H, HD, G = 4, 128, 1024, 8, 128, 3
T = B * S
J = G * H * HD
EPS = 1e-6


def setup_inputs():
    s = mx_kscale(T).reshape(B, S, 1)
    u = mx_kscale(J)
    ug = u.reshape(G, H, HD)
    st = s[:, :, :, None]
    x0 = bf(np.random.standard_normal((B, S, D)))
    rms1_scale = bf(1.0 + 0.1 * np.random.standard_normal(D))
    w0 = bf(np.random.standard_normal((D, J)) / np.sqrt(D))
    grads = [bf(np.random.standard_normal((B, S, H, HD)) * np.exp2(np.random.randint(-6, 1, (B, S, 1, 1))) / st * ug[j])
             for j in range(G)]
    rstd = 1.0 / np.sqrt(np.mean(np.square(f64(x0)), axis=-1) + EPS)
    return {"x": bf(f64(x0) * s),
            "rms1_scale": rms1_scale,
            "w_qkv": bf(f64(w0) / u),
            "rstd": np.asarray(rstd, np.float32),
            "grad_0": grads[0], "grad_1": grads[1], "grad_2": grads[2]}


def reference(x, rms1_scale, w_qkv, rstd, grad_0, grad_1, grad_2):
    gain = f64(rms1_scale)
    r = f64(rstd).reshape(T, 1)
    xhat = f64(x).reshape(T, D) * r
    h = xhat * gain
    dz = np.concatenate([f64(grad_0).reshape(T, H * HD),
                         f64(grad_1).reshape(T, H * HD),
                         f64(grad_2).reshape(T, H * HD)], axis=1)
    dh = mxq(dz, 1, "e5m2") @ mxq(f64(w_qkv), 1, "e4m3").T
    dw = mxq(h, 0, "e4m3").T @ mxq(dz, 0, "e5m2")
    dgain = np.sum(dh * xhat, axis=0)
    dn = dh * gain
    dx = r * (dn - xhat * np.mean(dn * xhat, axis=1, keepdims=True))
    return dx.reshape(B, S, D), dgain, dw

@@ -1,0 +1,341 @@
+from contextlib import ExitStack
+
+import concourse.mybir as mybir
+from concourse.masks import make_identity
+
+F32 = mybir.dt.float32
+BF16 = mybir.dt.bfloat16
+U32 = mybir.dt.uint32
+U8 = mybir.dt.uint8
+E4M3X4 = mybir.dt.float8_e4m3fn_x4
+E5M2X4 = mybir.dt.float8_e5m2_x4
+ALU = mybir.AluOpType
+ACT = mybir.ActivationFunctionType
+
+P = 128
+T, D, J = 512, 1024, 3072
+SLOTS = 4
+CHUNK = 512
+HALF = 512
+CHUNKS = J // CHUNK
+FLOPS = 2 * 2 * T * D * J
+
+
+def tile_transformerblocktpu_pa_v_kernel(
+    tc, x, rms1_scale, w_qkv, rstd, grad_0, grad_1, grad_2, out_0, out_1, out_2
+):
+    nc = tc.nc
+    grads = [grad_0, grad_1, grad_2]
+
+    with ExitStack() as ctx:
+        keep = ctx.enter_context(tc.tile_pool(name="keep", bufs=1))
+        big = ctx.enter_context(tc.tile_pool(name="big", bufs=8))
+        grp_pool = ctx.enter_context(tc.tile_pool(name="grp", bufs=5))
+        grw_pool = ctx.enter_context(tc.tile_pool(name="grw", bufs=6))
+        st_pool = ctx.enter_context(tc.tile_pool(name="st", bufs=6))
+        ps_t = ctx.enter_context(tc.psum_pool(name="ps_t", bufs=4))
+        ps_a = ctx.enter_context(tc.psum_pool(name="ps_a", bufs=4))
+        ctx.enter_context(tc.manual_schedule())
+
+        def token_view(ap):
+            return ap.rearrange("(p j) w -> p j w", j=SLOTS)
+
+        x_hbm = token_view(x.rearrange("b s d -> (b s) d"))
+        dx_hbm = token_view(out_0.rearrange("b s d -> (b s) d"))
+        g_hbm = [token_view(g.rearrange("b s h d -> (b s) (h d)")) for g in grads]
+        r_hbm = rstd.rearrange("b s -> (b s)").rearrange("(p j) -> p j", j=SLOTS)
+
+        ident = keep.tile([P, P], F32, name="ident")
+        ones_b = keep.tile([P, P], BF16, name="ones_b")
+        ones_f = keep.tile([P, P], F32, name="ones_f")
+        gain_in = keep.tile([1, D], BF16, name="gain_in")
+        gain_row = keep.tile([P, D], BF16, name="gain_row")
+        gain_bc = keep.tile([P, D], F32, name="gain_bc")
+        warm = keep.tile([P, 1], F32, name="warm")
+        r_sb = keep.tile([P, SLOTS], F32, name="r_sb")
+        nr2 = keep.tile([P, SLOTS], F32, name="nr2")
+        s_sb = keep.tile([P, SLOTS], F32, name="s_sb")
+        negc = keep.tile([P, SLOTS], F32, name="negc")
+        p_acc = keep.tile([P, D], F32, name="p_acc")
+        dg_sb = keep.tile([P, D], F32, name="dg_sb")
+        rg = [keep.tile([P, SLOTS, HALF], F32, name="rg%d" % a) for a in range(2)]
+        xh = [keep.tile([P, SLOTS, HALF], BF16, name="xh%d" % a) for a in range(2)]
+        g0 = [keep.tile([P, SLOTS, CHUNK], BF16, name="g0_%d" % a) for a in range(2)]
+        g12 = [keep.tile([P, SLOTS, D], BF16, name="g12_%d" % a) for a in range(2)]
+        h_codes = keep.tile([P, D], U32, name="h_codes", align_bytes=64)
+        h_sc = keep.tile([P, D], U8, name="h_sc", align_bytes=64)
+        zt_codes = keep.tile([P, CHUNKS, CHUNK], U32, name="zt_codes", align_bytes=64)
+        zt_sc = keep.tile([P, CHUNKS, CHUNK], U8, name="zt_sc", align_bytes=64)
+        zf_codes = keep.tile([P, CHUNKS, T], U32, name="zf_codes", align_bytes=64)
+        zf_sc = keep.tile([P, CHUNKS, T], U8, name="zf_sc", align_bytes=64)
+        w_codes = keep.tile([P, 2, CHUNKS, HALF], U32, name="w_codes", align_bytes=64)
+        w_sc = keep.tile([P, 2, CHUNKS, HALF], U8, name="w_sc", align_bytes=64)
+        w_sb = [big.tile([P, J], BF16, name="w_sb%d" % i, tag="big") for i in range(8)]
+
+        nc.sync.dma_start(out=gain_in[:], in_=rms1_scale.rearrange("(o d) -> o d", o=1))
+        nc.sync.dma_start(out=r_sb[:], in_=r_hbm)
+        nc.vector.memset(gain_row[:], 0.0)
+        nc.vector.memset(ones_b[:], 1.0)
+        nc.vector.memset(warm[:], 0.0)
+        nc.scalar.activation(out=warm[:], in_=warm[:], func=ACT.Copy)
+        make_identity(nc, ident[:])
+        nc.gpsimd.memset(ones_f[:], 1.0)
+
+        for a in range(2):
+            nc.sync.dma_start(out=g0[a][:], in_=g_hbm[0][:, :, a * CHUNK : (a + 1) * CHUNK])
+        for a in range(2):
+            nc.sync.dma_start(out=xh[a][:], in_=x_hbm[:, :, a * HALF : (a + 1) * HALF])
+        for a in range(2):
+            nc.sync.dma_start(out=g12[a][:], in_=g_hbm[1 + a])
+        for i in range(8):
+            nc.sync.dma_start(out=w_sb[i][:], in_=w_qkv[i * P : (i + 1) * P, :])
+
+        def dz(c):
+            if c < 2:
+                return g0[c][:]
+            return g12[c // 2 - 1][:, :, (c % 2) * CHUNK : (c % 2 + 1) * CHUNK]
+
+        def copy_out(engine, out, in_):
+            if engine == "v":
+                nc.vector.tensor_copy(out=out, in_=in_)
+            else:
+                nc.scalar.copy(out=out, in_=in_)
+
+        def transpose_bank(rows):
+            bank = ps_t.tile([P, 2, 2, P], F32, name="bank", tag="t")
+            for r in range(2):
+                for u in range(2):
+                    nc.tensor.transpose(bank[:, r, u, :], rows[r][:, u : 2 * P : 2], ident[:])
+            return bank
+
+        def bank_out(engine, bank, grp):
+            copy_out(
+                engine,
+                grp.bitcast(F32).rearrange("p (r d u) -> p r d u", r=2, u=2),
+                bank[:].rearrange("p r u d -> p r d u"),
+            )
+
+        def transpose_dz(c):
+            return [
+                transpose_bank([dz(c)[:, 2 * q + r, :].bitcast(F32) for r in range(2)])
+                for q in range(2)
+            ]
+
+        def dz_features_out(engines, banks):
+            grp = grp_pool.tile([P, SLOTS * T], BF16, name="grp", tag="grp", align_bytes=64)
+            for q in range(2):
+                bank_out(engines[q], banks[q], grp[:, q * 1024 : (q + 1) * 1024])
+            return grp
+
+        def quantize_dz_features(c, grp):
+            nc.vector.quantize_mx(
+                out=zf_codes[:, c, :].bitcast(E5M2X4), scales=zf_sc[:, c, :], in_=grp[:]
+            )
+
+        def interleave_dz(c):
+            grp = grp_pool.tile([P, SLOTS * CHUNK], BF16, name="grp", tag="grp", align_bytes=64)
+            nc.vector.tensor_copy(
+                out=grp[:].rearrange("p (w j) -> p w j", j=SLOTS),
+                in_=dz(c).rearrange("p j w -> p w j"),
+            )
+            return grp
+
+        def quantize_dz_tokens(c, grp):
+            nc.vector.quantize_mx(
+                out=zt_codes[:, c, :].bitcast(E5M2X4), scales=zt_sc[:, c, :], in_=grp[:]
+            )
+
+        def scale_factors(a, bank):
+            for j in range(SLOTS):
+                nc.scalar.activation(
+                    out=rg[a][:, j, :], in_=bank[:], func=ACT.Copy, scale=r_sb[:, j : j + 1]
+                )
+
+        def make_h(a):
+            grp = grp_pool.tile([P, SLOTS * HALF], BF16, name="grp", tag="grp", align_bytes=64)
+            nc.vector.tensor_tensor(
+                out=grp[:].rearrange("p (w j) -> p w j", j=SLOTS),
+                in0=xh[a][:].rearrange("p j w -> p w j"),
+                in1=rg[a][:].rearrange("p j w -> p w j"),
+                op=ALU.mult,
+            )
+            return grp
+
+        def quantize_h(a, grp):
+            cols = slice(a * HALF, (a + 1) * HALF)
+            nc.vector.quantize_mx(
+                out=h_codes[:, cols].bitcast(E4M3X4), scales=h_sc[:, cols], in_=grp[:]
+            )
+
+        def transpose_w(i, g):
+            return transpose_bank(
+                [
+                    w_sb[2 * i + r][:].bitcast(F32)[:, g * 2 * P : (g + 1) * 2 * P]
+                    for r in range(2)
+                ]
+            )
+
+        def w_out(engine, bank):
+            grp = grw_pool.tile([P, 1024], BF16, name="grw", tag="grw", align_bytes=64)
+            bank_out(engine, bank, grp[:])
+            return grp
+
+        def quantize_w(i, g, grp):
+            cols = slice((i % 2) * 256, (i % 2 + 1) * 256)
+            nc.vector.quantize_mx(
+                out=w_codes[:, i // 2, g, cols].bitcast(E4M3X4),
+                scales=w_sc[:, i // 2, g, cols],
+                in_=grp[:],
+            )
+
+        def dw_unit(gi, m, engines="ss"):
+            st = st_pool.tile([P, D], F32, name="st", tag="st")
+            m_cols = slice(m * P, (m + 1) * P)
+            banks = []
+            for e in range(2):
+                acc = ps_a.tile([P, CHUNK], F32, name="acc", tag="a")
+                nc.tensor.matmul_mx(
+                    out=acc[:],
+                    lhsT=h_codes[:, m_cols].bitcast(E4M3X4),
+                    lhsT_scale=h_sc[:, m_cols],
+                    rhs=zt_codes[:, 2 * gi + e, :].bitcast(E5M2X4),
+                    rhs_scale=zt_sc[:, 2 * gi + e, :],
+                    start=True,
+                    stop=True,
+                )
+                banks.append(acc)
+            for e in range(2):
+                copy_out(engines[e], st[:, e * CHUNK : (e + 1) * CHUNK], banks[e][:])
+            nc.sync.dma_start(out=out_2[m * P : (m + 1) * P, gi * D : (gi + 1) * D], in_=st[:])
+
+        def dh_group(j, half):
+            acc = ps_t.tile([P, HALF], F32, name="bank", tag="t")
+            tok = slice(j * P, (j + 1) * P)
+            for g in range(CHUNKS):
+                nc.tensor.matmul_mx(
+                    out=acc[:],
+                    lhsT=zf_codes[:, g, tok].bitcast(E5M2X4),
+                    lhsT_scale=zf_sc[:, g, tok],
+                    rhs=w_codes[:, half, g, :].bitcast(E4M3X4),
+                    rhs_scale=w_sc[:, half, g, :],
+                    start=(g == 0),
+                    stop=(g == CHUNKS - 1),
+                )
+            return acc
+
+        nc.vector.tensor_copy(out=gain_row[0:1, :], in_=gain_in[:])
+        gain_banks = []
+        for a in range(2):
+            gb = ps_a.tile([P, HALF], F32, name="acc", tag="a")
+            nc.tensor.matmul(
+                gb[:], ones_b[:], gain_row[:, a * HALF : (a + 1) * HALF], start=True, stop=True
+            )
+            gain_banks.append(gb)
+        scale_factors(0, gain_banks[0])
+        for a in range(2):
+            nc.vector.tensor_copy(out=gain_bc[:, a * HALF : (a + 1) * HALF], in_=gain_banks[a][:])
+        nc.vector.scalar_tensor_tensor(
+            out=nr2[:], in0=r_sb[:], scalar=-1.0 / D, in1=r_sb[:], op0=ALU.mult, op1=ALU.mult
+        )
+
+        zb0 = transpose_dz(0)
+        it0 = interleave_dz(0)
+        zb1 = transpose_dz(1)
+        zg0 = dz_features_out("ss", zb0)
+        it1 = interleave_dz(1)
+        quantize_dz_tokens(0, it0)
+        ha = make_h(0)
+        zg1 = dz_features_out("ss", zb1)
+        scale_factors(1, gain_banks[1])
+        quantize_dz_tokens(1, it1)
+        quantize_h(0, ha)
+        quantize_dz_features(0, zg0)
+        hb = make_h(1)
+        quantize_dz_features(1, zg1)
+        quantize_h(1, hb)
+
+        for gi in (1, 2):
+            c0, c1 = 2 * gi, 2 * gi + 1
+            b0 = transpose_dz(c0)
+            b1 = transpose_dz(c1)
+            i0 = interleave_dz(c0)
+            i1 = interleave_dz(c1)
+            f0 = dz_features_out("ss", b0)
+            f1 = dz_features_out("ss", b1)
+            quantize_dz_tokens(c0, i0)
+            quantize_dz_tokens(c1, i1)
+            quantize_dz_features(c0, f0)
+            quantize_dz_features(c1, f1)
+            dw_unit(0, 2 * gi - 2)
+            dw_unit(0, 2 * gi - 1)
+
+        pending = []
+        for k in range(12):
+            i, pp = k // 3, k % 3
+            banks = [transpose_w(i, 2 * pp + e) for e in range(2)]
+            engines = "sv" if k >= 6 else "ss"
+            grps = [w_out(engines[e], banks[e]) for e in range(2)]
+            for args in pending:
+                quantize_w(*args)
+            pending = [(i, 2 * pp + e, grps[e]) for e in range(2)]
+            if pp == 1:
+                dw_unit(0, 4 + i)
+        for args in pending:
+            quantize_w(*args)
+
+        rest = [(gi, m) for gi in (1, 2) for m in range(8)]
+        p_sum = None
+        for j in range(SLOTS):
+            units = rest[4 * j : 4 * j + 4]
+            acc0 = dh_group(j, 0)
+            dw_unit(*units[0])
+            acc1 = dh_group(j, 1)
+            dw_unit(*units[1])
+            accs = [acc0, acc1]
+            r_j = r_sb[:, j : j + 1]
+            p_t = big.tile([P, D], F32, name="p_t", tag="big")
+            t_t = big.tile([P, D], F32, name="t_t", tag="big")
+            u_t = big.tile([P, D], F32, name="u_t", tag="big")
+            dx_t = big.tile([P, D], F32, name="dx_t", tag="big")
+            for a in range(2):
+                nc.vector.scalar_tensor_tensor(
+                    out=p_t[:, a * HALF : (a + 1) * HALF],
+                    in0=accs[a][:], scalar=r_j, in1=xh[a][:, j, :],
+                    op0=ALU.mult, op1=ALU.mult,
+                )
+            for a in range(2):
+                nc.vector.scalar_tensor_tensor(
+                    out=t_t[:, a * HALF : (a + 1) * HALF],
+                    in0=accs[a][:], scalar=r_j, in1=gain_bc[:, a * HALF : (a + 1) * HALF],
+                    op0=ALU.mult, op1=ALU.mult,
+                )
+            nc.vector.scalar_tensor_tensor(
+                out=u_t[:], in0=p_t[:], scalar=1.0, in1=gain_bc[:],
+                op0=ALU.mult, op1=ALU.mult, accum_out=s_sb[:, j : j + 1],
+            )
+            if j == 0:
+                p_sum = p_t
+            elif j < 3:
+                nc.vector.tensor_tensor(out=p_acc[:], in0=p_sum[:], in1=p_t[:], op=ALU.add)
+                p_sum = p_acc
+            nc.vector.tensor_tensor(
+                out=negc[:, j : j + 1], in0=s_sb[:, j : j + 1], in1=nr2[:, j : j + 1], op=ALU.mult
+            )
+            for a in range(2):
+                nc.vector.scalar_tensor_tensor(
+                    out=dx_t[:, a * HALF : (a + 1) * HALF],
+                    in0=xh[a][:, j, :], scalar=negc[:, j : j + 1],
+                    in1=t_t[:, a * HALF : (a + 1) * HALF],
+                    op0=ALU.mult, op1=ALU.add,
+                )
+            if j == 3:
+                for a in range(2):
+                    dgb = ps_t.tile([P, HALF], F32, name="bank", tag="t")
+                    cols = slice(a * HALF, (a + 1) * HALF)
+                    nc.tensor.matmul(dgb[:], ones_f[:], p_sum[:, cols], start=True, stop=False)
+                    nc.tensor.matmul(dgb[:], ones_f[:], p_t[:, cols], start=False, stop=True)
+                    nc.scalar.copy(out=dg_sb[:, cols], in_=dgb[:])
+            dw_unit(*units[2])
+            dw_unit(*units[3])
+            nc.sync.dma_start(out=dx_hbm[:, j, :], in_=dx_t[:])
+        nc.sync.dma_start(out=out_1.rearrange("(o d) -> o d", o=1), in_=dg_sb[0:1, :])

@@ -10,7 +10,7 @@ U8 = mybir.dt.uint8
 E4M3X4 = mybir.dt.float8_e4m3fn_x4
 E5M2X4 = mybir.dt.float8_e5m2_x4
 ALU = mybir.AluOpType
-ACT = mybir.ActivationFunctionType
+COPY = mybir.ActivationFunctionType.Copy
 
 P = 128
 T, D, J = 512, 1024, 3072
@@ -18,324 +18,390 @@ SLOTS = 4
 CHUNK = 512
 HALF = 512
 CHUNKS = J // CHUNK
+PAIR = 2 * P
+W_TILES = D // P
 FLOPS = 2 * 2 * T * D * J
+
+W_AHEAD = 6
+STRIPS_AFTER_RUN = (1, 1, 1, 1, 1, 1, 1, 1, 1, 1, 2, 2)
+FIRST_DH_RUN = 6
+STRIPS_AFTER_SLOT = (1, 1, 2, 2)
+SHARED_STRIPS = range(3, 8)
 
 
 def tile_transformerblocktpu_pa_v_kernel(
     tc, x, rms1_scale, w_qkv, rstd, grad_0, grad_1, grad_2, out_0, out_1, out_2
 ):
     nc = tc.nc
-    grads = [grad_0, grad_1, grad_2]
 
     with ExitStack() as ctx:
         keep = ctx.enter_context(tc.tile_pool(name="keep", bufs=1))
-        big = ctx.enter_context(tc.tile_pool(name="big", bufs=8))
-        grp_pool = ctx.enter_context(tc.tile_pool(name="grp", bufs=5))
-        grw_pool = ctx.enter_context(tc.tile_pool(name="grw", bufs=6))
-        st_pool = ctx.enter_context(tc.tile_pool(name="st", bufs=6))
-        ps_t = ctx.enter_context(tc.psum_pool(name="ps_t", bufs=4))
-        ps_a = ctx.enter_context(tc.psum_pool(name="ps_a", bufs=4))
+        table_pool = ctx.enter_context(tc.tile_pool(name="table_pool", bufs=2))
+        w_pool = ctx.enter_context(tc.tile_pool(name="w_pool", bufs=W_AHEAD))
+        dz_pool = ctx.enter_context(tc.tile_pool(name="dz_pool", bufs=6))
+        w_group_pool = ctx.enter_context(tc.tile_pool(name="w_group_pool", bufs=4))
+        row_pool = ctx.enter_context(tc.tile_pool(name="row_pool", bufs=7))
+        dump_pool = ctx.enter_context(tc.tile_pool(name="dump_pool", bufs=2))
+        product_pool = ctx.enter_context(tc.tile_pool(name="product_pool", bufs=4))
+        turn_psum = ctx.enter_context(tc.psum_pool(name="turn_psum", bufs=4))
+        strip_psum = ctx.enter_context(tc.psum_pool(name="strip_psum", bufs=4))
         ctx.enter_context(tc.manual_schedule())
 
-        def token_view(ap):
-            return ap.rearrange("(p j) w -> p j w", j=SLOTS)
+        def by_slot(rows):
+            return rows.rearrange("(p j) w -> p j w", j=SLOTS)
 
-        x_hbm = token_view(x.rearrange("b s d -> (b s) d"))
-        dx_hbm = token_view(out_0.rearrange("b s d -> (b s) d"))
-        g_hbm = [token_view(g.rearrange("b s h d -> (b s) (h d)")) for g in grads]
-        r_hbm = rstd.rearrange("b s -> (b s)").rearrange("(p j) -> p j", j=SLOTS)
+        x_hbm = by_slot(x.rearrange("b s d -> (b s) d"))
+        dx_hbm = by_slot(out_0.rearrange("b s d -> (b s) d"))
+        grads = (grad_0, grad_1, grad_2)
+        grad_hbm = [by_slot(g.rearrange("b s h d -> (b s) (h d)")) for g in grads]
+        rstd_hbm = rstd.rearrange("b s -> (b s)").rearrange("(p j) -> p j", j=SLOTS)
 
         ident = keep.tile([P, P], F32, name="ident")
-        ones_b = keep.tile([P, P], BF16, name="ones_b")
-        ones_f = keep.tile([P, P], F32, name="ones_f")
+        ones_bf16 = keep.tile([P, P], BF16, name="ones_bf16")
+        ones_f32 = keep.tile([P, P], F32, name="ones_f32")
         gain_in = keep.tile([1, D], BF16, name="gain_in")
         gain_row = keep.tile([P, D], BF16, name="gain_row")
-        gain_bc = keep.tile([P, D], F32, name="gain_bc")
+        gain = keep.tile([P, D], F32, name="gain")
         warm = keep.tile([P, 1], F32, name="warm")
-        r_sb = keep.tile([P, SLOTS], F32, name="r_sb")
-        nr2 = keep.tile([P, SLOTS], F32, name="nr2")
-        s_sb = keep.tile([P, SLOTS], F32, name="s_sb")
-        negc = keep.tile([P, SLOTS], F32, name="negc")
-        p_acc = keep.tile([P, D], F32, name="p_acc")
-        dg_sb = keep.tile([P, D], F32, name="dg_sb")
-        rg = [keep.tile([P, SLOTS, HALF], F32, name="rg%d" % a) for a in range(2)]
-        xh = [keep.tile([P, SLOTS, HALF], BF16, name="xh%d" % a) for a in range(2)]
-        g0 = [keep.tile([P, SLOTS, CHUNK], BF16, name="g0_%d" % a) for a in range(2)]
-        g12 = [keep.tile([P, SLOTS, D], BF16, name="g12_%d" % a) for a in range(2)]
+        r = keep.tile([P, SLOTS], F32, name="r")
+        minus_r2_d = keep.tile([P, SLOTS], F32, name="minus_r2_d")
+        row_sums = keep.tile([P, 2, SLOTS], F32, name="row_sums")
+        x_factor = keep.tile([P, SLOTS], F32, name="x_factor")
+        token_sum = keep.tile([P, HALF], F32, name="token_sum")
+        x_sb = keep.tile([P, SLOTS, D], BF16, name="x_sb")
+        grad_0_sb = [keep.tile([P, SLOTS, CHUNK], BF16, name="grad_0_sb%d" % e) for e in range(2)]
+        grad_12_sb = [keep.tile([P, SLOTS, D], BF16, name="grad_12_sb%d" % g) for g in range(2)]
         h_codes = keep.tile([P, D], U32, name="h_codes", align_bytes=64)
-        h_sc = keep.tile([P, D], U8, name="h_sc", align_bytes=64)
-        zt_codes = keep.tile([P, CHUNKS, CHUNK], U32, name="zt_codes", align_bytes=64)
-        zt_sc = keep.tile([P, CHUNKS, CHUNK], U8, name="zt_sc", align_bytes=64)
-        zf_codes = keep.tile([P, CHUNKS, T], U32, name="zf_codes", align_bytes=64)
-        zf_sc = keep.tile([P, CHUNKS, T], U8, name="zf_sc", align_bytes=64)
+        h_scales = keep.tile([P, D], U8, name="h_scales", align_bytes=64)
+        dz_tok_codes = keep.tile([P, CHUNKS, CHUNK], U32, name="dz_tok_codes", align_bytes=64)
+        dz_tok_scales = keep.tile([P, CHUNKS, CHUNK], U8, name="dz_tok_scales", align_bytes=64)
+        dz_feat_codes = keep.tile([P, CHUNKS, T], U32, name="dz_feat_codes", align_bytes=64)
+        dz_feat_scales = keep.tile([P, CHUNKS, T], U8, name="dz_feat_scales", align_bytes=64)
         w_codes = keep.tile([P, 2, CHUNKS, HALF], U32, name="w_codes", align_bytes=64)
-        w_sc = keep.tile([P, 2, CHUNKS, HALF], U8, name="w_sc", align_bytes=64)
-        w_sb = [big.tile([P, J], BF16, name="w_sb%d" % i, tag="big") for i in range(8)]
+        w_scales = keep.tile([P, 2, CHUNKS, HALF], U8, name="w_scales", align_bytes=64)
 
         nc.sync.dma_start(out=gain_in[:], in_=rms1_scale.rearrange("(o d) -> o d", o=1))
-        nc.sync.dma_start(out=r_sb[:], in_=r_hbm)
-        nc.vector.memset(gain_row[:], 0.0)
-        nc.vector.memset(ones_b[:], 1.0)
-        nc.vector.memset(warm[:], 0.0)
-        nc.scalar.activation(out=warm[:], in_=warm[:], func=ACT.Copy)
-        make_identity(nc, ident[:])
-        nc.gpsimd.memset(ones_f[:], 1.0)
+        nc.sync.dma_start(out=r[:], in_=rstd_hbm)
+        for e in range(2):
+            nc.sync.dma_start(
+                out=grad_0_sb[e][:], in_=grad_hbm[0][:, :, e * CHUNK : (e + 1) * CHUNK]
+            )
+        nc.sync.dma_start(out=x_sb[:], in_=x_hbm)
+        for g in range(2):
+            nc.sync.dma_start(out=grad_12_sb[g][:], in_=grad_hbm[1 + g])
 
-        for a in range(2):
-            nc.sync.dma_start(out=g0[a][:], in_=g_hbm[0][:, :, a * CHUNK : (a + 1) * CHUNK])
-        for a in range(2):
-            nc.sync.dma_start(out=xh[a][:], in_=x_hbm[:, :, a * HALF : (a + 1) * HALF])
-        for a in range(2):
-            nc.sync.dma_start(out=g12[a][:], in_=g_hbm[1 + a])
-        for i in range(8):
-            nc.sync.dma_start(out=w_sb[i][:], in_=w_qkv[i * P : (i + 1) * P, :])
+        w_sb = []
+
+        def load_w():
+            first = len(w_sb) * P
+            tile = w_pool.tile([P, J], BF16, name="w_tile")
+            nc.sync.dma_start(out=tile[:], in_=w_qkv[first : first + P, :])
+            w_sb.append(tile)
+
+        for n in range(W_AHEAD):
+            load_w()
+
+        nc.vector.memset(gain_row[:], 0.0)
+        nc.vector.memset(ones_bf16[:], 1.0)
+        nc.vector.memset(warm[:], 0.0)
+        nc.scalar.activation(out=warm[:], in_=warm[:], func=COPY)
+        make_identity(nc, ident[:])
+        nc.gpsimd.memset(ones_f32[:], 1.0)
+
+        def turn(rows):
+            bank = turn_psum.tile([P, 2, 2, P], F32, name="turned", tag="turn")
+            for v in range(2):
+                for u in range(2):
+                    nc.tensor.transpose(bank[:, v, u, :], rows[v][:, u : 2 * P : 2], ident[:])
+            return bank
+
+        def copy_turned(bank, group):
+            nc.scalar.copy(
+                out=group.bitcast(F32).rearrange("p (v q u) -> p v q u", v=2, u=2),
+                in_=bank[:].rearrange("p v u q -> p v q u"),
+            )
+
+        dz_by_token = {}
+        dz_by_feature = {}
 
         def dz(c):
             if c < 2:
-                return g0[c][:]
-            return g12[c // 2 - 1][:, :, (c % 2) * CHUNK : (c % 2 + 1) * CHUNK]
+                return grad_0_sb[c][:]
+            return grad_12_sb[c // 2 - 1][:, :, (c % 2) * CHUNK : (c % 2 + 1) * CHUNK]
 
-        def copy_out(engine, out, in_):
-            if engine == "v":
-                nc.vector.tensor_copy(out=out, in_=in_)
-            else:
-                nc.scalar.copy(out=out, in_=in_)
-
-        def transpose_bank(rows):
-            bank = ps_t.tile([P, 2, 2, P], F32, name="bank", tag="t")
-            for r in range(2):
-                for u in range(2):
-                    nc.tensor.transpose(bank[:, r, u, :], rows[r][:, u : 2 * P : 2], ident[:])
-            return bank
-
-        def bank_out(engine, bank, grp):
-            copy_out(
-                engine,
-                grp.bitcast(F32).rearrange("p (r d u) -> p r d u", r=2, u=2),
-                bank[:].rearrange("p r u d -> p r d u"),
-            )
-
-        def transpose_dz(c):
-            return [
-                transpose_bank([dz(c)[:, 2 * q + r, :].bitcast(F32) for r in range(2)])
-                for q in range(2)
+        def turn_dz(c):
+            group = dz_pool.tile([P, SLOTS * T], BF16, name="group", tag="dz", align_bytes=64)
+            banks = [
+                turn([dz(c)[:, 2 * q + v, :].bitcast(F32) for v in range(2)]) for q in range(2)
             ]
-
-        def dz_features_out(engines, banks):
-            grp = grp_pool.tile([P, SLOTS * T], BF16, name="grp", tag="grp", align_bytes=64)
             for q in range(2):
-                bank_out(engines[q], banks[q], grp[:, q * 1024 : (q + 1) * 1024])
-            return grp
+                copy_turned(banks[q], group[:, q * 1024 : (q + 1) * 1024])
+            dz_by_feature[c] = group
 
-        def quantize_dz_features(c, grp):
+        def quantize_features(c):
             nc.vector.quantize_mx(
-                out=zf_codes[:, c, :].bitcast(E5M2X4), scales=zf_sc[:, c, :], in_=grp[:]
+                out=dz_feat_codes[:, c, :].bitcast(E5M2X4),
+                scales=dz_feat_scales[:, c, :],
+                in_=dz_by_feature[c][:],
             )
 
-        def interleave_dz(c):
-            grp = grp_pool.tile([P, SLOTS * CHUNK], BF16, name="grp", tag="grp", align_bytes=64)
+        def interleave_tokens(c):
+            group = dz_pool.tile([P, SLOTS * CHUNK], BF16, name="group", tag="dz", align_bytes=64)
             nc.vector.tensor_copy(
-                out=grp[:].rearrange("p (w j) -> p w j", j=SLOTS),
-                in_=dz(c).rearrange("p j w -> p w j"),
+                out=group[:].rearrange("p (f i j) -> p f j i", i=4, j=SLOTS),
+                in_=dz(c).rearrange("p j (f i) -> p f j i", i=4),
             )
-            return grp
+            dz_by_token[c] = group
 
-        def quantize_dz_tokens(c, grp):
+        def quantize_tokens(c):
             nc.vector.quantize_mx(
-                out=zt_codes[:, c, :].bitcast(E5M2X4), scales=zt_sc[:, c, :], in_=grp[:]
+                out=dz_tok_codes[:, c, :].bitcast(E5M2X4),
+                scales=dz_tok_scales[:, c, :],
+                in_=dz_by_token[c][:],
             )
 
-        def scale_factors(a, bank):
+        r_gain = [
+            table_pool.tile([P, SLOTS, HALF], F32, name="r_gain%d" % a, tag="table")
+            for a in range(2)
+        ]
+
+        def make_table(a, gain_bank):
             for j in range(SLOTS):
                 nc.scalar.activation(
-                    out=rg[a][:, j, :], in_=bank[:], func=ACT.Copy, scale=r_sb[:, j : j + 1]
+                    out=r_gain[a][:, j, :], in_=gain_bank[:], func=COPY, scale=r[:, j : j + 1]
                 )
 
         def make_h(a):
-            grp = grp_pool.tile([P, SLOTS * HALF], BF16, name="grp", tag="grp", align_bytes=64)
+            group = dz_pool.tile([P, SLOTS * HALF], BF16, name="group", tag="dz", align_bytes=64)
+            x_half = x_sb[:, :, a * HALF : (a + 1) * HALF]
             nc.vector.tensor_tensor(
-                out=grp[:].rearrange("p (w j) -> p w j", j=SLOTS),
-                in0=xh[a][:].rearrange("p j w -> p w j"),
-                in1=rg[a][:].rearrange("p j w -> p w j"),
+                out=group[:].rearrange("p (f i j) -> p f j i", i=4, j=SLOTS),
+                in0=x_half.rearrange("p j (f i) -> p f j i", i=4),
+                in1=r_gain[a][:].rearrange("p j (f i) -> p f j i", i=4),
                 op=ALU.mult,
             )
-            return grp
+            return group
 
-        def quantize_h(a, grp):
+        def quantize_h(a, group):
             cols = slice(a * HALF, (a + 1) * HALF)
             nc.vector.quantize_mx(
-                out=h_codes[:, cols].bitcast(E4M3X4), scales=h_sc[:, cols], in_=grp[:]
+                out=h_codes[:, cols].bitcast(E4M3X4), scales=h_scales[:, cols], in_=group[:]
             )
 
-        def transpose_w(i, g):
-            return transpose_bank(
-                [
-                    w_sb[2 * i + r][:].bitcast(F32)[:, g * 2 * P : (g + 1) * 2 * P]
-                    for r in range(2)
-                ]
-            )
+        def turn_w(i, c):
+            words = slice(c * CHUNK // 2, (c + 1) * CHUNK // 2)
+            bank = turn([w_sb[2 * i + v][:].bitcast(F32)[:, words] for v in range(2)])
+            group = w_group_pool.tile([P, PAIR * 4], BF16, name="w_group", align_bytes=64)
+            copy_turned(bank, group[:])
+            return group
 
-        def w_out(engine, bank):
-            grp = grw_pool.tile([P, 1024], BF16, name="grw", tag="grw", align_bytes=64)
-            bank_out(engine, bank, grp[:])
-            return grp
-
-        def quantize_w(i, g, grp):
-            cols = slice((i % 2) * 256, (i % 2 + 1) * 256)
+        def quantize_w(i, c, group):
+            cols = slice((i % 2) * PAIR, (i % 2 + 1) * PAIR)
             nc.vector.quantize_mx(
-                out=w_codes[:, i // 2, g, cols].bitcast(E4M3X4),
-                scales=w_sc[:, i // 2, g, cols],
-                in_=grp[:],
+                out=w_codes[:, i // 2, c, cols].bitcast(E4M3X4),
+                scales=w_scales[:, i // 2, c, cols],
+                in_=group[:],
             )
 
-        def dw_unit(gi, m, engines="ss"):
-            st = st_pool.tile([P, D], F32, name="st", tag="st")
-            m_cols = slice(m * P, (m + 1) * P)
-            banks = []
-            for e in range(2):
-                acc = ps_a.tile([P, CHUNK], F32, name="acc", tag="a")
-                nc.tensor.matmul_mx(
-                    out=acc[:],
-                    lhsT=h_codes[:, m_cols].bitcast(E4M3X4),
-                    lhsT_scale=h_sc[:, m_cols],
-                    rhs=zt_codes[:, 2 * gi + e, :].bitcast(E5M2X4),
-                    rhs_scale=zt_sc[:, 2 * gi + e, :],
-                    start=True,
-                    stop=True,
-                )
-                banks.append(acc)
-            for e in range(2):
-                copy_out(engines[e], st[:, e * CHUNK : (e + 1) * CHUNK], banks[e][:])
-            nc.sync.dma_start(out=out_2[m * P : (m + 1) * P, gi * D : (gi + 1) * D], in_=st[:])
+        strips = [(g, m) for g in range(3) for m in range(D // P)]
+        strips_done = []
 
-        def dh_group(j, half):
-            acc = ps_t.tile([P, HALF], F32, name="bank", tag="t")
-            tok = slice(j * P, (j + 1) * P)
-            for g in range(CHUNKS):
-                nc.tensor.matmul_mx(
-                    out=acc[:],
-                    lhsT=zf_codes[:, g, tok].bitcast(E5M2X4),
-                    lhsT_scale=zf_sc[:, g, tok],
-                    rhs=w_codes[:, half, g, :].bitcast(E4M3X4),
-                    rhs_scale=w_sc[:, half, g, :],
-                    start=(g == 0),
-                    stop=(g == CHUNKS - 1),
+        def next_strips(count):
+            for n in range(count):
+                index = len(strips_done)
+                g, m = strips[index]
+                strips_done.append(index)
+                rows = row_pool.tile([P, D], F32, name="rows", tag="rows")
+                h_cols = slice(m * P, (m + 1) * P)
+                banks = []
+                for e in range(2):
+                    bank = strip_psum.tile([P, CHUNK], F32, name="sums", tag="sums")
+                    nc.tensor.matmul_mx(
+                        out=bank[:],
+                        lhsT=h_codes[:, h_cols].bitcast(E4M3X4),
+                        lhsT_scale=h_scales[:, h_cols],
+                        rhs=dz_tok_codes[:, 2 * g + e, :].bitcast(E5M2X4),
+                        rhs_scale=dz_tok_scales[:, 2 * g + e, :],
+                        start=True,
+                        stop=True,
+                    )
+                    banks.append(bank)
+                nc.scalar.copy(out=rows[:, :CHUNK], in_=banks[0][:])
+                if index in SHARED_STRIPS:
+                    nc.vector.tensor_copy(out=rows[:, CHUNK:], in_=banks[1][:])
+                else:
+                    nc.scalar.copy(out=rows[:, CHUNK:], in_=banks[1][:])
+                nc.sync.dma_start(
+                    out=out_2[m * P : (m + 1) * P, g * D : (g + 1) * D], in_=rows[:]
                 )
-            return acc
+
+        rg_dh = []
+
+        def dh_sums(j, a, bank):
+            tokens = slice(j * P, (j + 1) * P)
+            for c in range(CHUNKS):
+                nc.tensor.matmul_mx(
+                    out=bank[:],
+                    lhsT=dz_feat_codes[:, c, tokens].bitcast(E5M2X4),
+                    lhsT_scale=dz_feat_scales[:, c, tokens],
+                    rhs=w_codes[:, a, c, :].bitcast(E4M3X4),
+                    rhs_scale=w_scales[:, a, c, :],
+                    start=(c == 0),
+                    stop=(c == CHUNKS - 1),
+                )
+
+        def times_xhat(j, a, bank):
+            product = product_pool.tile([P, HALF], F32, name="product")
+            nc.vector.scalar_tensor_tensor(
+                out=product[:], in0=bank[:], scalar=r[:, j : j + 1],
+                in1=x_sb[:, j, a * HALF : (a + 1) * HALF], op0=ALU.mult, op1=ALU.mult,
+            )
+            return product
+
+        def times_gain(j, a, bank):
+            cols = slice(a * HALF, (a + 1) * HALF)
+            nc.vector.scalar_tensor_tensor(
+                out=rg_dh[j // 2][:, j % 2, cols], in0=bank[:], scalar=r[:, j : j + 1],
+                in1=gain[:, cols], op0=ALU.mult, op1=ALU.mult,
+            )
+
+        def sum_row(j, a, product):
+            dump = dump_pool.tile([P, HALF], F32, name="dump")
+            nc.vector.scalar_tensor_tensor(
+                out=dump[:], in0=product[:], scalar=1.0, in1=gain[:, a * HALF : (a + 1) * HALF],
+                op0=ALU.mult, op1=ALU.mult, accum_out=row_sums[:, a, j : j + 1],
+            )
+
+        def find_x_factor(j):
+            nc.vector.tensor_scalar(
+                out=x_factor[:, j : j + 1], in0=row_sums[:, 0, j : j + 1],
+                scalar1=row_sums[:, 1, j : j + 1], scalar2=minus_r2_d[:, j : j + 1],
+                op0=ALU.add, op1=ALU.mult,
+            )
+
+        def finish_dx(j, pieces):
+            rows = row_pool.tile([P, D], F32, name="rows", tag="rows")
+            for n in range(pieces):
+                cols = slice(n * D // pieces, (n + 1) * D // pieces)
+                nc.vector.scalar_tensor_tensor(
+                    out=rows[:, cols], in0=x_sb[:, j, cols], scalar=x_factor[:, j : j + 1],
+                    in1=rg_dh[j // 2][:, j % 2, cols], op0=ALU.mult, op1=ALU.add,
+                )
+                nc.sync.dma_start(out=dx_hbm[:, j, cols], in_=rows[:, cols])
+
+        def sum_partitions(bank, part, first, last):
+            nc.tensor.matmul(bank[:], ones_f32[:], part[:], start=first, stop=last)
 
         nc.vector.tensor_copy(out=gain_row[0:1, :], in_=gain_in[:])
         gain_banks = []
         for a in range(2):
-            gb = ps_a.tile([P, HALF], F32, name="acc", tag="a")
+            bank = strip_psum.tile([P, HALF], F32, name="sums", tag="sums")
             nc.tensor.matmul(
-                gb[:], ones_b[:], gain_row[:, a * HALF : (a + 1) * HALF], start=True, stop=True
+                bank[:], ones_bf16[:], gain_row[:, a * HALF : (a + 1) * HALF], start=True, stop=True
             )
-            gain_banks.append(gb)
-        scale_factors(0, gain_banks[0])
-        for a in range(2):
-            nc.vector.tensor_copy(out=gain_bc[:, a * HALF : (a + 1) * HALF], in_=gain_banks[a][:])
+            gain_banks.append(bank)
+        make_table(0, gain_banks[0])
         nc.vector.scalar_tensor_tensor(
-            out=nr2[:], in0=r_sb[:], scalar=-1.0 / D, in1=r_sb[:], op0=ALU.mult, op1=ALU.mult
+            out=minus_r2_d[:], in0=r[:], scalar=-1.0 / D, in1=r[:], op0=ALU.mult, op1=ALU.mult
         )
 
-        zb0 = transpose_dz(0)
-        it0 = interleave_dz(0)
-        zb1 = transpose_dz(1)
-        zg0 = dz_features_out("ss", zb0)
-        it1 = interleave_dz(1)
-        quantize_dz_tokens(0, it0)
-        ha = make_h(0)
-        zg1 = dz_features_out("ss", zb1)
-        scale_factors(1, gain_banks[1])
-        quantize_dz_tokens(1, it1)
-        quantize_h(0, ha)
-        quantize_dz_features(0, zg0)
-        hb = make_h(1)
-        quantize_dz_features(1, zg1)
-        quantize_h(1, hb)
+        interleave_tokens(0)
+        turn_dz(0)
+        turn_dz(1)
+        interleave_tokens(1)
+        quantize_tokens(0)
+        h_0 = make_h(0)
+        make_table(1, gain_banks[1])
+        for a in range(2):
+            nc.scalar.copy(out=gain[:, a * HALF : (a + 1) * HALF], in_=gain_banks[a][:])
+        quantize_tokens(1)
+        quantize_h(0, h_0)
+        h_1 = make_h(1)
+        quantize_features(0)
+        quantize_h(1, h_1)
+        quantize_features(1)
 
-        for gi in (1, 2):
-            c0, c1 = 2 * gi, 2 * gi + 1
-            b0 = transpose_dz(c0)
-            b1 = transpose_dz(c1)
-            i0 = interleave_dz(c0)
-            i1 = interleave_dz(c1)
-            f0 = dz_features_out("ss", b0)
-            f1 = dz_features_out("ss", b1)
-            quantize_dz_tokens(c0, i0)
-            quantize_dz_tokens(c1, i1)
-            quantize_dz_features(c0, f0)
-            quantize_dz_features(c1, f1)
-            dw_unit(0, 2 * gi - 2)
-            dw_unit(0, 2 * gi - 1)
+        turn_dz(2)
+        interleave_tokens(2)
+        interleave_tokens(3)
+        next_strips(1)
+        turn_dz(3)
+        quantize_tokens(2)
+        quantize_tokens(3)
+        next_strips(1)
+        turn_dz(4)
+        quantize_features(2)
+        next_strips(1)
+        turn_dz(5)
+        quantize_features(3)
+        next_strips(1)
 
-        pending = []
+        rest_of_dz = {
+            0: [(quantize_features, 4)],
+            1: [(quantize_features, 5)],
+            6: [(interleave_tokens, 4)],
+            7: [(interleave_tokens, 5), (quantize_tokens, 4)],
+            8: [(quantize_tokens, 5)],
+        }
+        products_0 = []
+
+        def add_up_half_0(j):
+            sum_row(j, 0, products_0[j])
+            if j > 0:
+                so_far = products_0[0] if j == 1 else token_sum
+                nc.vector.tensor_tensor(
+                    out=token_sum[:], in0=so_far[:], in1=products_0[j][:], op=ALU.add
+                )
+
+        turned = []
         for k in range(12):
-            i, pp = k // 3, k % 3
-            banks = [transpose_w(i, 2 * pp + e) for e in range(2)]
-            engines = "sv" if k >= 6 else "ss"
-            grps = [w_out(engines[e], banks[e]) for e in range(2)]
-            for args in pending:
-                quantize_w(*args)
-            pending = [(i, 2 * pp + e, grps[e]) for e in range(2)]
-            if pp == 1:
-                dw_unit(0, 4 + i)
-        for args in pending:
-            quantize_w(*args)
+            if k == 3:
+                load_w()
+                load_w()
+            run = [(k // 3, 2 * (k % 3) + e) for e in range(2)]
+            groups = [turn_w(i, c) for i, c in run]
+            for i, c, group in turned:
+                quantize_w(i, c, group)
+            for step, c in rest_of_dz.get(k, []):
+                step(c)
+            j = k - FIRST_DH_RUN
+            if 0 <= j < SLOTS:
+                if j == 0:
+                    for n in range(2):
+                        rg_dh_tile = table_pool.tile([P, 2, D], F32, name="rg_dh", tag="table")
+                        rg_dh.append(rg_dh_tile)
+                bank = strip_psum.tile([P, HALF], F32, name="sums", tag="sums")
+                dh_sums(j, 0, bank)
+                products_0.append(times_xhat(j, 0, bank))
+                times_gain(j, 0, bank)
+            if 1 <= j <= SLOTS:
+                add_up_half_0(j - 1)
+            next_strips(STRIPS_AFTER_RUN[k])
+            turned = [(i, c, group) for (i, c), group in zip(run, groups)]
+        for i, c, group in turned:
+            quantize_w(i, c, group)
 
-        rest = [(gi, m) for gi in (1, 2) for m in range(8)]
-        p_sum = None
+        products_1 = []
         for j in range(SLOTS):
-            units = rest[4 * j : 4 * j + 4]
-            acc0 = dh_group(j, 0)
-            dw_unit(*units[0])
-            acc1 = dh_group(j, 1)
-            dw_unit(*units[1])
-            accs = [acc0, acc1]
-            r_j = r_sb[:, j : j + 1]
-            p_t = big.tile([P, D], F32, name="p_t", tag="big")
-            t_t = big.tile([P, D], F32, name="t_t", tag="big")
-            u_t = big.tile([P, D], F32, name="u_t", tag="big")
-            dx_t = big.tile([P, D], F32, name="dx_t", tag="big")
-            for a in range(2):
-                nc.vector.scalar_tensor_tensor(
-                    out=p_t[:, a * HALF : (a + 1) * HALF],
-                    in0=accs[a][:], scalar=r_j, in1=xh[a][:, j, :],
-                    op0=ALU.mult, op1=ALU.mult,
-                )
-            for a in range(2):
-                nc.vector.scalar_tensor_tensor(
-                    out=t_t[:, a * HALF : (a + 1) * HALF],
-                    in0=accs[a][:], scalar=r_j, in1=gain_bc[:, a * HALF : (a + 1) * HALF],
-                    op0=ALU.mult, op1=ALU.mult,
-                )
-            nc.vector.scalar_tensor_tensor(
-                out=u_t[:], in0=p_t[:], scalar=1.0, in1=gain_bc[:],
-                op0=ALU.mult, op1=ALU.mult, accum_out=s_sb[:, j : j + 1],
-            )
-            if j == 0:
-                p_sum = p_t
-            elif j < 3:
-                nc.vector.tensor_tensor(out=p_acc[:], in0=p_sum[:], in1=p_t[:], op=ALU.add)
-                p_sum = p_acc
-            nc.vector.tensor_tensor(
-                out=negc[:, j : j + 1], in0=s_sb[:, j : j + 1], in1=nr2[:, j : j + 1], op=ALU.mult
-            )
-            for a in range(2):
-                nc.vector.scalar_tensor_tensor(
-                    out=dx_t[:, a * HALF : (a + 1) * HALF],
-                    in0=xh[a][:, j, :], scalar=negc[:, j : j + 1],
-                    in1=t_t[:, a * HALF : (a + 1) * HALF],
-                    op0=ALU.mult, op1=ALU.add,
-                )
-            if j == 3:
-                for a in range(2):
-                    dgb = ps_t.tile([P, HALF], F32, name="bank", tag="t")
-                    cols = slice(a * HALF, (a + 1) * HALF)
-                    nc.tensor.matmul(dgb[:], ones_f[:], p_sum[:, cols], start=True, stop=False)
-                    nc.tensor.matmul(dgb[:], ones_f[:], p_t[:, cols], start=False, stop=True)
-                    nc.scalar.copy(out=dg_sb[:, cols], in_=dgb[:])
-            dw_unit(*units[2])
-            dw_unit(*units[3])
-            nc.sync.dma_start(out=dx_hbm[:, j, :], in_=dx_t[:])
-        nc.sync.dma_start(out=out_1.rearrange("(o d) -> o d", o=1), in_=dg_sb[0:1, :])
+            bank = turn_psum.tile([P, HALF], F32, name="turned", tag="turn")
+            dh_sums(j, 1, bank)
+            next_strips(STRIPS_AFTER_SLOT[j])
+            products_1.append(times_xhat(j, 1, bank))
+            if j > 0:
+                find_x_factor(j - 1)
+            times_gain(j, 1, bank)
+            if j > 0:
+                finish_dx(j - 1, 1)
+            sum_row(j, 1, products_1[j])
+
+        find_x_factor(SLOTS - 1)
+        finish_dx(SLOTS - 1, 2)
+        sums_0 = turn_psum.tile([P, HALF], F32, name="turned", tag="turn")
+        sum_partitions(sums_0, token_sum, True, True)
+        sums_1 = turn_psum.tile([P, HALF], F32, name="turned", tag="turn")
+        for j in range(SLOTS):
+            sum_partitions(sums_1, products_1[j], j == 0, j == SLOTS - 1)
+        out_1_rows = row_pool.tile([P, D], F32, name="rows", tag="rows")
+        nc.scalar.copy(out=out_1_rows[:, :HALF], in_=sums_0[:])
+        nc.scalar.copy(out=out_1_rows[:, HALF:], in_=sums_1[:])
+        nc.sync.dma_start(out=out_1.rearrange("(o d) -> o d", o=1), in_=out_1_rows[0:1, :])

from contextlib import ExitStack

import concourse.mybir as mybir
from concourse.masks import make_identity

F32 = mybir.dt.float32
BF16 = mybir.dt.bfloat16
U32 = mybir.dt.uint32
U8 = mybir.dt.uint8
E4M3X4 = mybir.dt.float8_e4m3fn_x4
E5M2X4 = mybir.dt.float8_e5m2_x4
ALU = mybir.AluOpType
COPY = mybir.ActivationFunctionType.Copy

P = 128
T, D, J = 512, 1024, 3072
SLOTS = 4
CHUNK = 512
HALF = 512
CHUNKS = J // CHUNK
PAIR = 2 * P
W_TILES = D // P
FLOPS = 2 * 2 * T * D * J

W_AHEAD = 6
STRIPS_AFTER_RUN = (1, 1, 1, 1, 1, 1, 1, 1, 1, 1, 2, 2)
FIRST_DH_RUN = 6
STRIPS_AFTER_SLOT = (1, 1, 2, 2)
SHARED_STRIPS = range(3, 8)


def tile_transformerblocktpu_pa_v_kernel(
    tc, x, rms1_scale, w_qkv, rstd, grad_0, grad_1, grad_2, out_0, out_1, out_2
):
    nc = tc.nc

    with ExitStack() as ctx:
        keep = ctx.enter_context(tc.tile_pool(name="keep", bufs=1))
        table_pool = ctx.enter_context(tc.tile_pool(name="table_pool", bufs=2))
        w_pool = ctx.enter_context(tc.tile_pool(name="w_pool", bufs=W_AHEAD))
        dz_pool = ctx.enter_context(tc.tile_pool(name="dz_pool", bufs=6))
        w_group_pool = ctx.enter_context(tc.tile_pool(name="w_group_pool", bufs=4))
        row_pool = ctx.enter_context(tc.tile_pool(name="row_pool", bufs=7))
        dump_pool = ctx.enter_context(tc.tile_pool(name="dump_pool", bufs=2))
        product_pool = ctx.enter_context(tc.tile_pool(name="product_pool", bufs=4))
        turn_psum = ctx.enter_context(tc.psum_pool(name="turn_psum", bufs=4))
        strip_psum = ctx.enter_context(tc.psum_pool(name="strip_psum", bufs=4))
        ctx.enter_context(tc.manual_schedule())

        def by_slot(rows):
            return rows.rearrange("(p j) w -> p j w", j=SLOTS)

        x_hbm = by_slot(x.rearrange("b s d -> (b s) d"))
        dx_hbm = by_slot(out_0.rearrange("b s d -> (b s) d"))
        grads = (grad_0, grad_1, grad_2)
        grad_hbm = [by_slot(g.rearrange("b s h d -> (b s) (h d)")) for g in grads]
        rstd_hbm = rstd.rearrange("b s -> (b s)").rearrange("(p j) -> p j", j=SLOTS)

        ident = keep.tile([P, P], F32, name="ident")
        ones_bf16 = keep.tile([P, P], BF16, name="ones_bf16")
        ones_f32 = keep.tile([P, P], F32, name="ones_f32")
        gain_in = keep.tile([1, D], BF16, name="gain_in")
        gain_row = keep.tile([P, D], BF16, name="gain_row")
        gain = keep.tile([P, D], F32, name="gain")
        warm = keep.tile([P, 1], F32, name="warm")
        r = keep.tile([P, SLOTS], F32, name="r")
        minus_r2_d = keep.tile([P, SLOTS], F32, name="minus_r2_d")
        row_sums = keep.tile([P, 2, SLOTS], F32, name="row_sums")
        x_factor = keep.tile([P, SLOTS], F32, name="x_factor")
        token_sum = keep.tile([P, HALF], F32, name="token_sum")
        x_sb = keep.tile([P, SLOTS, D], BF16, name="x_sb")
        grad_0_sb = [keep.tile([P, SLOTS, CHUNK], BF16, name="grad_0_sb%d" % e) for e in range(2)]
        grad_12_sb = [keep.tile([P, SLOTS, D], BF16, name="grad_12_sb%d" % g) for g in range(2)]
        h_codes = keep.tile([P, D], U32, name="h_codes", align_bytes=64)
        h_scales = keep.tile([P, D], U8, name="h_scales", align_bytes=64)
        dz_tok_codes = keep.tile([P, CHUNKS, CHUNK], U32, name="dz_tok_codes", align_bytes=64)
        dz_tok_scales = keep.tile([P, CHUNKS, CHUNK], U8, name="dz_tok_scales", align_bytes=64)
        dz_feat_codes = keep.tile([P, CHUNKS, T], U32, name="dz_feat_codes", align_bytes=64)
        dz_feat_scales = keep.tile([P, CHUNKS, T], U8, name="dz_feat_scales", align_bytes=64)
        w_codes = keep.tile([P, 2, CHUNKS, HALF], U32, name="w_codes", align_bytes=64)
        w_scales = keep.tile([P, 2, CHUNKS, HALF], U8, name="w_scales", align_bytes=64)

        nc.sync.dma_start(out=gain_in[:], in_=rms1_scale.rearrange("(o d) -> o d", o=1))
        nc.sync.dma_start(out=r[:], in_=rstd_hbm)
        for e in range(2):
            nc.sync.dma_start(
                out=grad_0_sb[e][:], in_=grad_hbm[0][:, :, e * CHUNK : (e + 1) * CHUNK]
            )
        nc.sync.dma_start(out=x_sb[:], in_=x_hbm)
        for g in range(2):
            nc.sync.dma_start(out=grad_12_sb[g][:], in_=grad_hbm[1 + g])

        w_sb = []

        def load_w():
            first = len(w_sb) * P
            tile = w_pool.tile([P, J], BF16, name="w_tile")
            nc.sync.dma_start(out=tile[:], in_=w_qkv[first : first + P, :])
            w_sb.append(tile)

        for n in range(W_AHEAD):
            load_w()

        nc.vector.memset(gain_row[:], 0.0)
        nc.vector.memset(ones_bf16[:], 1.0)
        nc.vector.memset(warm[:], 0.0)
        nc.scalar.activation(out=warm[:], in_=warm[:], func=COPY)
        make_identity(nc, ident[:])
        nc.gpsimd.memset(ones_f32[:], 1.0)

        def turn(rows):
            bank = turn_psum.tile([P, 2, 2, P], F32, name="turned", tag="turn")
            for v in range(2):
                for u in range(2):
                    nc.tensor.transpose(bank[:, v, u, :], rows[v][:, u : 2 * P : 2], ident[:])
            return bank

        def copy_turned(bank, group):
            nc.scalar.copy(
                out=group.bitcast(F32).rearrange("p (v q u) -> p v q u", v=2, u=2),
                in_=bank[:].rearrange("p v u q -> p v q u"),
            )

        dz_by_token = {}
        dz_by_feature = {}

        def dz(c):
            if c < 2:
                return grad_0_sb[c][:]
            return grad_12_sb[c // 2 - 1][:, :, (c % 2) * CHUNK : (c % 2 + 1) * CHUNK]

        def turn_dz(c):
            group = dz_pool.tile([P, SLOTS * T], BF16, name="group", tag="dz", align_bytes=64)
            banks = [
                turn([dz(c)[:, 2 * q + v, :].bitcast(F32) for v in range(2)]) for q in range(2)
            ]
            for q in range(2):
                copy_turned(banks[q], group[:, q * 1024 : (q + 1) * 1024])
            dz_by_feature[c] = group

        def quantize_features(c):
            nc.vector.quantize_mx(
                out=dz_feat_codes[:, c, :].bitcast(E5M2X4),
                scales=dz_feat_scales[:, c, :],
                in_=dz_by_feature[c][:],
            )

        def interleave_tokens(c):
            group = dz_pool.tile([P, SLOTS * CHUNK], BF16, name="group", tag="dz", align_bytes=64)
            nc.vector.tensor_copy(
                out=group[:].rearrange("p (f i j) -> p f j i", i=4, j=SLOTS),
                in_=dz(c).rearrange("p j (f i) -> p f j i", i=4),
            )
            dz_by_token[c] = group

        def quantize_tokens(c):
            nc.vector.quantize_mx(
                out=dz_tok_codes[:, c, :].bitcast(E5M2X4),
                scales=dz_tok_scales[:, c, :],
                in_=dz_by_token[c][:],
            )

        r_gain = [
            table_pool.tile([P, SLOTS, HALF], F32, name="r_gain%d" % a, tag="table")
            for a in range(2)
        ]

        def make_table(a, gain_bank):
            for j in range(SLOTS):
                nc.scalar.activation(
                    out=r_gain[a][:, j, :], in_=gain_bank[:], func=COPY, scale=r[:, j : j + 1]
                )

        def make_h(a):
            group = dz_pool.tile([P, SLOTS * HALF], BF16, name="group", tag="dz", align_bytes=64)
            x_half = x_sb[:, :, a * HALF : (a + 1) * HALF]
            nc.vector.tensor_tensor(
                out=group[:].rearrange("p (f i j) -> p f j i", i=4, j=SLOTS),
                in0=x_half.rearrange("p j (f i) -> p f j i", i=4),
                in1=r_gain[a][:].rearrange("p j (f i) -> p f j i", i=4),
                op=ALU.mult,
            )
            return group

        def quantize_h(a, group):
            cols = slice(a * HALF, (a + 1) * HALF)
            nc.vector.quantize_mx(
                out=h_codes[:, cols].bitcast(E4M3X4), scales=h_scales[:, cols], in_=group[:]
            )

        def turn_w(i, c):
            words = slice(c * CHUNK // 2, (c + 1) * CHUNK // 2)
            bank = turn([w_sb[2 * i + v][:].bitcast(F32)[:, words] for v in range(2)])
            group = w_group_pool.tile([P, PAIR * 4], BF16, name="w_group", align_bytes=64)
            copy_turned(bank, group[:])
            return group

        def quantize_w(i, c, group):
            cols = slice((i % 2) * PAIR, (i % 2 + 1) * PAIR)
            nc.vector.quantize_mx(
                out=w_codes[:, i // 2, c, cols].bitcast(E4M3X4),
                scales=w_scales[:, i // 2, c, cols],
                in_=group[:],
            )

        strips = [(g, m) for g in range(3) for m in range(D // P)]
        strips_done = []

        def next_strips(count):
            for n in range(count):
                index = len(strips_done)
                g, m = strips[index]
                strips_done.append(index)
                rows = row_pool.tile([P, D], F32, name="rows", tag="rows")
                h_cols = slice(m * P, (m + 1) * P)
                banks = []
                for e in range(2):
                    bank = strip_psum.tile([P, CHUNK], F32, name="sums", tag="sums")
                    nc.tensor.matmul_mx(
                        out=bank[:],
                        lhsT=h_codes[:, h_cols].bitcast(E4M3X4),
                        lhsT_scale=h_scales[:, h_cols],
                        rhs=dz_tok_codes[:, 2 * g + e, :].bitcast(E5M2X4),
                        rhs_scale=dz_tok_scales[:, 2 * g + e, :],
                        start=True,
                        stop=True,
                    )
                    banks.append(bank)
                nc.scalar.copy(out=rows[:, :CHUNK], in_=banks[0][:])
                if index in SHARED_STRIPS:
                    nc.vector.tensor_copy(out=rows[:, CHUNK:], in_=banks[1][:])
                else:
                    nc.scalar.copy(out=rows[:, CHUNK:], in_=banks[1][:])
                nc.sync.dma_start(
                    out=out_2[m * P : (m + 1) * P, g * D : (g + 1) * D], in_=rows[:]
                )

        rg_dh = []

        def dh_sums(j, a, bank):
            tokens = slice(j * P, (j + 1) * P)
            for c in range(CHUNKS):
                nc.tensor.matmul_mx(
                    out=bank[:],
                    lhsT=dz_feat_codes[:, c, tokens].bitcast(E5M2X4),
                    lhsT_scale=dz_feat_scales[:, c, tokens],
                    rhs=w_codes[:, a, c, :].bitcast(E4M3X4),
                    rhs_scale=w_scales[:, a, c, :],
                    start=(c == 0),
                    stop=(c == CHUNKS - 1),
                )

        def times_xhat(j, a, bank):
            product = product_pool.tile([P, HALF], F32, name="product")
            nc.vector.scalar_tensor_tensor(
                out=product[:], in0=bank[:], scalar=r[:, j : j + 1],
                in1=x_sb[:, j, a * HALF : (a + 1) * HALF], op0=ALU.mult, op1=ALU.mult,
            )
            return product

        def times_gain(j, a, bank):
            cols = slice(a * HALF, (a + 1) * HALF)
            nc.vector.scalar_tensor_tensor(
                out=rg_dh[j // 2][:, j % 2, cols], in0=bank[:], scalar=r[:, j : j + 1],
                in1=gain[:, cols], op0=ALU.mult, op1=ALU.mult,
            )

        def sum_row(j, a, product):
            dump = dump_pool.tile([P, HALF], F32, name="dump")
            nc.vector.scalar_tensor_tensor(
                out=dump[:], in0=product[:], scalar=1.0, in1=gain[:, a * HALF : (a + 1) * HALF],
                op0=ALU.mult, op1=ALU.mult, accum_out=row_sums[:, a, j : j + 1],
            )

        def find_x_factor(j):
            nc.vector.tensor_scalar(
                out=x_factor[:, j : j + 1], in0=row_sums[:, 0, j : j + 1],
                scalar1=row_sums[:, 1, j : j + 1], scalar2=minus_r2_d[:, j : j + 1],
                op0=ALU.add, op1=ALU.mult,
            )

        def finish_dx(j, pieces):
            rows = row_pool.tile([P, D], F32, name="rows", tag="rows")
            for n in range(pieces):
                cols = slice(n * D // pieces, (n + 1) * D // pieces)
                nc.vector.scalar_tensor_tensor(
                    out=rows[:, cols], in0=x_sb[:, j, cols], scalar=x_factor[:, j : j + 1],
                    in1=rg_dh[j // 2][:, j % 2, cols], op0=ALU.mult, op1=ALU.add,
                )
                nc.sync.dma_start(out=dx_hbm[:, j, cols], in_=rows[:, cols])

        def sum_partitions(bank, part, first, last):
            nc.tensor.matmul(bank[:], ones_f32[:], part[:], start=first, stop=last)

        nc.vector.tensor_copy(out=gain_row[0:1, :], in_=gain_in[:])
        gain_banks = []
        for a in range(2):
            bank = strip_psum.tile([P, HALF], F32, name="sums", tag="sums")
            nc.tensor.matmul(
                bank[:], ones_bf16[:], gain_row[:, a * HALF : (a + 1) * HALF], start=True, stop=True
            )
            gain_banks.append(bank)
        make_table(0, gain_banks[0])
        nc.vector.scalar_tensor_tensor(
            out=minus_r2_d[:], in0=r[:], scalar=-1.0 / D, in1=r[:], op0=ALU.mult, op1=ALU.mult
        )

        interleave_tokens(0)
        turn_dz(0)
        turn_dz(1)
        interleave_tokens(1)
        quantize_tokens(0)
        h_0 = make_h(0)
        make_table(1, gain_banks[1])
        for a in range(2):
            nc.scalar.copy(out=gain[:, a * HALF : (a + 1) * HALF], in_=gain_banks[a][:])
        quantize_tokens(1)
        quantize_h(0, h_0)
        h_1 = make_h(1)
        quantize_features(0)
        quantize_h(1, h_1)
        quantize_features(1)

        turn_dz(2)
        interleave_tokens(2)
        interleave_tokens(3)
        next_strips(1)
        turn_dz(3)
        quantize_tokens(2)
        quantize_tokens(3)
        next_strips(1)
        turn_dz(4)
        quantize_features(2)
        next_strips(1)
        turn_dz(5)
        quantize_features(3)
        next_strips(1)

        rest_of_dz = {
            0: [(quantize_features, 4)],
            1: [(quantize_features, 5)],
            6: [(interleave_tokens, 4)],
            7: [(interleave_tokens, 5), (quantize_tokens, 4)],
            8: [(quantize_tokens, 5)],
        }
        products_0 = []

        def add_up_half_0(j):
            sum_row(j, 0, products_0[j])
            if j > 0:
                so_far = products_0[0] if j == 1 else token_sum
                nc.vector.tensor_tensor(
                    out=token_sum[:], in0=so_far[:], in1=products_0[j][:], op=ALU.add
                )

        turned = []
        for k in range(12):
            if k == 3:
                load_w()
                load_w()
            run = [(k // 3, 2 * (k % 3) + e) for e in range(2)]
            groups = [turn_w(i, c) for i, c in run]
            for i, c, group in turned:
                quantize_w(i, c, group)
            for step, c in rest_of_dz.get(k, []):
                step(c)
            j = k - FIRST_DH_RUN
            if 0 <= j < SLOTS:
                if j == 0:
                    for n in range(2):
                        rg_dh_tile = table_pool.tile([P, 2, D], F32, name="rg_dh", tag="table")
                        rg_dh.append(rg_dh_tile)
                bank = strip_psum.tile([P, HALF], F32, name="sums", tag="sums")
                dh_sums(j, 0, bank)
                products_0.append(times_xhat(j, 0, bank))
                times_gain(j, 0, bank)
            if 1 <= j <= SLOTS:
                add_up_half_0(j - 1)
            next_strips(STRIPS_AFTER_RUN[k])
            turned = [(i, c, group) for (i, c), group in zip(run, groups)]
        for i, c, group in turned:
            quantize_w(i, c, group)

        products_1 = []
        for j in range(SLOTS):
            bank = turn_psum.tile([P, HALF], F32, name="turned", tag="turn")
            dh_sums(j, 1, bank)
            next_strips(STRIPS_AFTER_SLOT[j])
            products_1.append(times_xhat(j, 1, bank))
            if j > 0:
                find_x_factor(j - 1)
            times_gain(j, 1, bank)
            if j > 0:
                finish_dx(j - 1, 1)
            sum_row(j, 1, products_1[j])

        find_x_factor(SLOTS - 1)
        finish_dx(SLOTS - 1, 2)
        sums_0 = turn_psum.tile([P, HALF], F32, name="turned", tag="turn")
        sum_partitions(sums_0, token_sum, True, True)
        sums_1 = turn_psum.tile([P, HALF], F32, name="turned", tag="turn")
        for j in range(SLOTS):
            sum_partitions(sums_1, products_1[j], j == 0, j == SLOTS - 1)
        out_1_rows = row_pool.tile([P, D], F32, name="rows", tag="rows")
        nc.scalar.copy(out=out_1_rows[:, :HALF], in_=sums_0[:])
        nc.scalar.copy(out=out_1_rows[:, HALF:], in_=sums_1[:])
        nc.sync.dma_start(out=out_1.rearrange("(o d) -> o d", o=1), in_=out_1_rows[0:1, :])
